import numpy as np
import ml_dtypes


def mxq(x, axis, fmt="e4m3"):
    dtype, down = {"e4m3": (ml_dtypes.float8_e4m3fn, 7), "e5m2": (ml_dtypes.float8_e5m2, 14)}[fmt]
    v = np.moveaxis(np.asarray(x, np.float32).astype(ml_dtypes.bfloat16).astype(np.float64), axis, -1)
    blocks = v.reshape(v.shape[:-1] + (-1, 32))
    amax = np.abs(blocks).max(-1, keepdims=True)
    byte = np.maximum(np.where(amax > 0, np.frexp(amax)[1] - 1 + 127, 0) - down, 1)
    scale = np.exp2(byte - 127.0)
    codes = (blocks / scale).astype(np.float32).astype(dtype).astype(np.float64)
    return np.moveaxis((codes * scale).reshape(v.shape), -1, axis)


WIDE = False


def mx_kscale(k):
    if not WIDE:
        return np.ones(k)
    levels = np.array([10, -10, 5, -5, 0])
    if k % 512:
        return np.exp2(np.random.permutation(np.resize(levels, k // 32))).repeat(32)
    a = np.empty((k // 512, 16))
    for p in range(k // 512):
        a[p, :8] = np.random.permutation(np.resize(levels, 8))
        for g in range(8):
            far = levels[np.abs(levels - a[p, g]) >= 10]
            a[p, g + 8] = far[np.random.randint(len(far))]
    return np.exp2(a.ravel()).repeat(32)


BF16 = ml_dtypes.bfloat16


def bf(x):
    return np.asarray(x, np.float32).astype(BF16)


def f64(x):
    return np.asarray(x).astype(np.float64)


B, S, E, H, D, XL, TOPK = 2, 256, 1024, 8, 128, 512, 8
HD = H * D


def l2norm(x):
    return x / np.maximum(np.sqrt((x * x).sum(-1, keepdims=True)), 1e-12)


def split_heads(x):
    return x.reshape(B, S, H, D).transpose(0, 2, 1, 3)


def setup_inputs():
    n = np.random.standard_normal
    s = mx_kscale(E)
    return {"input": bf(n((B, S, E)) * s),
            "Wq": bf(n((HD, E)) / np.sqrt(E) / s), "bq": bf(n(HD) * 0.1),
            "Wk": bf(n((HD, E)) / np.sqrt(E) / s), "bk": bf(n(HD) * 0.1),
            "Wv": bf(n((HD, E)) / np.sqrt(E) / s), "bv": bf(n(HD) * 0.1)}


def reference(input, Wq, bq, Wk, bk, Wv, bv):
    xq = mxq(f64(input), 2, "e4m3")
    q = split_heads(l2norm((xq @ mxq(f64(Wq), 1, "e4m3").T) + f64(bq)))
    k = split_heads(l2norm((xq @ mxq(f64(Wk), 1, "e4m3").T) + f64(bk)))
    v = split_heads((xq @ mxq(f64(Wv), 1, "e4m3").T) + f64(bv))
    return q, k, v

@@ -1,0 +1,323 @@
+from contextlib import ExitStack
+
+import concourse.mybir as mybir
+from concourse.masks import make_identity
+
+FLOPS = 2 * 512 * 1024 * 3072
+
+FP8X4 = mybir.dt.float8_e4m3fn_x4
+F32 = mybir.dt.float32
+BF16 = mybir.dt.bfloat16
+U32 = mybir.dt.uint32
+U8 = mybir.dt.uint8
+I32 = mybir.dt.int32
+ALU = mybir.AluOpType
+ACT = mybir.ActivationFunctionType
+
+P = 128
+E = 1024
+NBLK = 512
+
+KB = (-98.5, -96.5, -93.5)
+BC = ("V", "V", "V")
+VE = {0: (1, 3), 1: (1,)}
+RE = "GGGGGGGG"
+TL = 1.5
+EL = 0.6
+QL = 1.5
+AL = 0.6
+SL = 2.0
+NL = 3.0
+RL = 4.0
+NWARM = 4
+BUFS = {"tp": 4, "acc": 4, "grp": 3}
+
+
+def tile_knnxlmultiheadsattention_pa_kernel(
+    tc, x_in, wq, bq, wk, bk, wv, bv, out_q, out_k, out_v
+):
+    nc = tc.nc
+    weights = (wq, wk, wv)
+    biases = (bq, bk, bv)
+    outs = (out_q, out_k, out_v)
+    with ExitStack() as ctx:
+        ctx.enter_context(tc.manual_schedule())
+        const = ctx.enter_context(tc.tile_pool(name="const", bufs=1))
+        raw = ctx.enter_context(tc.tile_pool(name="raw", bufs=1))
+        grp = ctx.enter_context(tc.tile_pool(name="grp", bufs=BUFS["grp"]))
+        keep = ctx.enter_context(tc.tile_pool(name="keep", bufs=1))
+        res = ctx.enter_context(tc.tile_pool(name="res", bufs=1))
+        scr = ctx.enter_context(tc.tile_pool(name="scr", bufs=2))
+        small = ctx.enter_context(tc.tile_pool(name="small", bufs=1))
+        tpp = ctx.enter_context(tc.psum_pool(name="tpp", bufs=BUFS["tp"]))
+        accp = ctx.enter_context(tc.psum_pool(name="accp", bufs=BUFS["acc"]))
+
+        ones = const.tile([P, NBLK], BF16, name="ones")
+        nc.gpsimd.memset(ones[:], 1.0)
+
+        bzs = []
+        for w in range(3):
+            bz = const.tile([P, E], BF16, name="bz%d" % w)
+            nc.vector.memset(bz[:].bitcast(I32), 0)
+            nc.scalar.dma_start(out=bz[0:1, :], in_=biases[w].rearrange("(o n) -> o n", o=1))
+            bzs.append(bz)
+
+        rows = []
+        xr = []
+        for tt in range(4):
+            b, jj = divmod(tt, 2)
+            t = raw.tile([P, E], BF16, name="xraw%d" % tt)
+            nc.sync.dma_start(out=t[:], in_=x_in[b].rearrange("(p j) e -> p j e", j=2)[:, jj, :])
+            xr.append(t[:])
+        rows.append(xr)
+        for w in range(3):
+            for c in range(2):
+                wsrc = weights[w][c * NBLK : (c + 1) * NBLK, :].rearrange("(p r) k -> p r k", r=4)
+                wr = []
+                for hf in range(2):
+                    t = raw.tile([P, 2, E], BF16, name="wraw%d%d%d" % (w, c, hf))
+                    nc.sync.dma_start(out=t[:], in_=wsrc[:, 2 * hf : 2 * hf + 2, :])
+                    wr.extend([t[:, 0, :], t[:, 1, :]])
+                rows.append(wr)
+
+        ident = const.tile([P, P], F32, name="ident")
+        make_identity(nc, ident[:])
+        mhalf = small.tile([P, 1], F32, name="mhalf")
+        nc.gpsimd.memset(mhalf[:], -0.5)
+        one2 = small.tile([P, 1], F32, name="one2")
+        nc.scalar.activation(out=one2[:], in_=mhalf[:], func=ACT.Square)
+
+        ops = {}
+        queues = {"PE": [], "V": [], "S": [], "G": [], "SP": []}
+
+        def add(eng, key, name, deps, emit, takes=(), frees=()):
+            ops[name] = (deps, emit, takes, frees)
+            queues[eng].append((key, len(ops), name))
+
+        tiles = {}
+
+        def copy_on(eng, out, in_):
+            if eng == "V":
+                nc.vector.tensor_copy(out=out, in_=in_)
+            else:
+                nc.scalar.copy(out=out, in_=in_)
+
+        def emit_bmm(w):
+            pb = accp.tile([P, E], BF16, tag="acc", name="pb%d" % w)
+            tiles[("pb", w)] = pb
+            for c in range(2):
+                nc.tensor.matmul(
+                    out=pb[:, c * NBLK : (c + 1) * NBLK],
+                    lhsT=ones[:, 0:P],
+                    rhs=bzs[w][:, c * NBLK : (c + 1) * NBLK],
+                    start=True,
+                    stop=True,
+                )
+
+        def emit_bc(w):
+            bb = const.tile([P, E], BF16, name="bias%d" % w)
+            tiles[("bias", w)] = bb
+            copy_on(BC[w], bb[:], tiles[("pb", w)][:])
+
+        def emit_warm(n):
+            pd = accp.tile([P, NBLK], F32, tag="acc", name="warm")
+            for k in range(n):
+                nc.tensor.matmul(out=pd[:], lhsT=ones[:, 0:P], rhs=ones[:], start=True, stop=True)
+
+        add("PE", -101.0, "D0", (), lambda: emit_warm(NWARM), takes=("acc",), frees=("acc",))
+
+        for w in range(3):
+            add("PE", KB[w], "bmm%d" % w, (), lambda w=w: emit_bmm(w), takes=("acc",))
+            add(BC[w], KB[w] + 0.3, "bc%d" % w, ("bmm%d" % w,), lambda w=w: emit_bc(w), frees=("acc",))
+
+        def emit_t(blk, r):
+            if r == 0:
+                tiles[("g4", blk)] = grp.tile(
+                    [P, 2, NBLK, 4], BF16, tag="g4", name="g4_%d" % blk, align_bytes=64
+                )
+            tp = tpp.tile([P, 2, 2, P], F32, tag="tp", name="tp%d_%d" % (blk, r))
+            tiles[("tp", blk, r)] = tp
+            src = rows[blk][r].bitcast(F32)
+            for g in range(2):
+                for u in range(2):
+                    nc.tensor.transpose(
+                        tp[:, g, u, :], src[:, 256 * g + u : 256 * (g + 1) : 2], ident[:]
+                    )
+
+        def emit_e(blk, r, eng):
+            gw = tiles[("g4", blk)][:].bitcast(F32)
+            copy_on(
+                eng,
+                gw[:, :, r * P : (r + 1) * P, :],
+                tiles[("tp", blk, r)][:].rearrange("p g u r -> p g r u"),
+            )
+
+        def emit_q(blk, g):
+            if g == 0:
+                tiles[("cd", blk)] = keep.tile([P, 2, NBLK], U32, name="cd%d" % blk, align_bytes=64)
+                tiles[("pl", blk)] = keep.tile([P, 2, NBLK], U8, name="pl%d" % blk, align_bytes=64)
+            nc.vector.quantize_mx(
+                out=tiles[("cd", blk)][:, g, :].bitcast(FP8X4),
+                scales=tiles[("pl", blk)][:, g, :],
+                in_=tiles[("g4", blk)][:, g, :, :].rearrange("p f t -> p (f t)"),
+            )
+
+        for blk in range(7):
+            for r in range(4):
+                if blk <= 2:
+                    kt = -100.0 + 4 * blk + r
+                    ke = kt + 0.1
+                else:
+                    j = 4 * (blk - 3) + r
+                    kt = 2 * (j // 2) + 0.01 * (j % 2) + TL
+                    ke = kt + EL
+                eng = "V" if r in VE.get(blk, ()) else "S"
+                add(
+                    "PE", kt, "T%d.%d" % (blk, r), (), lambda blk=blk, r=r: emit_t(blk, r),
+                    takes=("tp", "grp") if r == 0 else ("tp",),
+                )
+                add(
+                    eng, ke, "E%d.%d" % (blk, r), ("T%d.%d" % (blk, r),),
+                    lambda blk=blk, r=r, eng=eng: emit_e(blk, r, eng), frees=("tp",),
+                )
+            for g in range(2):
+                add(
+                    "V", ke + QL + 0.1 * g, "Q%d.%d" % (blk, g), tuple("E%d.%d" % (blk, r) for r in range(4)),
+                    lambda blk=blk, g=g: emit_q(blk, g), frees=("grp",) if g == 1 else (),
+                )
+
+        def emit_m(blk, tt):
+            acc = accp.tile([P, NBLK], F32, tag="acc", name="acc%d_%d" % (blk, tt))
+            tiles[("acc", blk, tt)] = acc
+            for g in range(2):
+                nc.tensor.matmul_mx(
+                    out=acc[:],
+                    lhsT=tiles[("cd", 0)][:, g, tt * P : (tt + 1) * P].bitcast(FP8X4),
+                    lhsT_scale=tiles[("pl", 0)][:, g, tt * P : (tt + 1) * P],
+                    rhs=tiles[("cd", blk)][:, g, :].bitcast(FP8X4),
+                    rhs_scale=tiles[("pl", blk)][:, g, :],
+                    start=(g == 0),
+                    stop=(g == 1),
+                )
+
+        def emit_a(blk, tt):
+            w, c = divmod(blk - 1, 2)
+            b, jj = divmod(tt, 2)
+            if (w, b) not in tiles:
+                tiles[(w, b)] = res.tile([P, 8, 2, P], F32, name="o%d%d" % (w, b))
+            y = tiles[(w, b)][:, 4 * c : 4 * c + 4, jj, :]
+            nc.vector.tensor_tensor(
+                out=y.rearrange("p h (e r) -> p h e r", r=4),
+                in0=tiles[("acc", blk, tt)][:].rearrange("p (r h e) -> p h e r", r=4, h=4),
+                in1=tiles[("bias", w)][:, c * NBLK : (c + 1) * NBLK].rearrange(
+                    "p (h e r) -> p h e r", h=4, r=4
+                ),
+                op=ALU.add,
+            )
+
+        def emit_sq(blk, tt):
+            w, c = divmod(blk - 1, 2)
+            b, jj = divmod(tt, 2)
+            if ("ss", w) not in tiles:
+                tiles[("ss", w)] = small.tile([P, 4, 2], F32, name="ss%d" % w)
+            junk = scr.tile([P, 4, P], F32, tag="junk", name="junk%d_%d" % (blk, tt))
+            nc.scalar.activation(
+                out=junk[:], in_=tiles[(w, b)][:, 4 * c : 4 * c + 4, jj, :], func=ACT.Square,
+                accum_out=tiles[("ss", w)][:, tt, c : c + 1],
+            )
+
+        def emit_n(w, tt):
+            ss = tiles[("ss", w)]
+            n2 = small.tile([P, 1], F32, name="n2_%d%d" % (w, tt))
+            nc.gpsimd.tensor_tensor(out=n2[:], in0=ss[:, tt, 0:1], in1=ss[:, tt, 1:2], op=ALU.add)
+            m2 = small.tile([P, 1], F32, name="m2_%d%d" % (w, tt))
+            nc.gpsimd.tensor_scalar(out=m2[:], in0=n2[:], scalar1=1e-24, scalar2=None, op0=ALU.max)
+            r2 = small.tile([P, 1], F32, name="r2_%d%d" % (w, tt))
+            tiles[("r2", w, tt)] = r2
+            nc.gpsimd.tensor_tensor(out=r2[:], in0=m2[:], in1=mhalf[:], op=ALU.pow)
+
+        def emit_r(w, tt, eng):
+            b, jj = divmod(tt, 2)
+            y = tiles[(w, b)][:, :, jj, :]
+            rr = tiles[("r2", w, tt)][:]
+            if eng == "V":
+                nc.vector.tensor_scalar(out=y, in0=y, scalar1=rr, scalar2=None, op0=ALU.mult)
+            elif eng == "G":
+                nc.gpsimd.tensor_scalar(out=y, in0=y, scalar1=rr, scalar2=0.0, op0=ALU.mult, op1=ALU.add)
+            else:
+                nc.scalar.activation(out=y, in_=y, func=ACT.Copy, scale=rr)
+
+        def emit_store(w, b, h0, h1):
+            nc.sync.dma_start(
+                out=outs[w][b, h0:h1].rearrange("h (p j) d -> p h (j d)", j=2),
+                in_=tiles[(w, b)][:, h0:h1, :, :].rearrange("p h j d -> p h (j d)"),
+            )
+
+        for i in range(24):
+            blk, tt = 1 + i // 4, i % 4
+            w = (blk - 1) // 2
+            add(
+                "PE", float(i), "M%d.%d" % (blk, tt), ("Q0.0", "Q0.1", "Q%d.0" % blk, "Q%d.1" % blk),
+                lambda blk=blk, tt=tt: emit_m(blk, tt), takes=("acc",),
+            )
+            add(
+                "V", i + AL, "A%d.%d" % (blk, tt), ("M%d.%d" % (blk, tt), "bc%d" % w),
+                lambda blk=blk, tt=tt: emit_a(blk, tt), frees=("acc",),
+            )
+            if w < 2:
+                add(
+                    "S", i + SL, "Sq%d.%d" % (blk, tt), ("A%d.%d" % (blk, tt),),
+                    lambda blk=blk, tt=tt: emit_sq(blk, tt),
+                )
+        for w in range(2):
+            for tt in range(4):
+                i = 8 * w + 4 + tt
+                add(
+                    "G", i + NL, "N%d.%d" % (w, tt), ("Sq%d.%d" % (2 * w + 1, tt), "Sq%d.%d" % (2 * w + 2, tt)),
+                    lambda w=w, tt=tt: emit_n(w, tt),
+                )
+                eng = RE[4 * w + tt]
+                add(
+                    eng, i + RL, "R%d.%d" % (w, tt), ("N%d.%d" % (w, tt),),
+                    lambda w=w, tt=tt, eng=eng: emit_r(w, tt, eng),
+                )
+            for b in range(2):
+                for c in range(2):
+                    add(
+                        "SP", 8 * w + 4 + 2 * b + 6 + 0.1 * c, "St%d%d%d" % (w, b, c),
+                        ("R%d.%d" % (w, 2 * b), "R%d.%d" % (w, 2 * b + 1)),
+                        lambda w=w, b=b, c=c: emit_store(w, b, 4 * c, 4 * c + 4),
+                    )
+        for c in range(2):
+            for b in range(2):
+                add(
+                    "SP", 16.0 + 4 * c + 2 * b + 2.5, "Stv%d%d" % (c, b),
+                    ("A%d.%d" % (5 + c, 2 * b), "A%d.%d" % (5 + c, 2 * b + 1)),
+                    lambda c=c, b=b: emit_store(2, b, 4 * c, 4 * c + 4),
+                )
+
+        order = {e: [n for (k, i, n) in sorted(q)] for e, q in queues.items()}
+        head = {e: 0 for e in order}
+        done = set()
+        held = {"tp": 0, "acc": 0, "grp": 0}
+        left = len(ops)
+        while left:
+            moved = False
+            for e in ("PE", "S", "V", "G", "SP"):
+                while head[e] < len(order[e]):
+                    name = order[e][head[e]]
+                    deps, emit, takes, frees = ops[name]
+                    if not all(d in done for d in deps):
+                        break
+                    if not all(held[p] < BUFS[p] for p in takes):
+                        break
+                    emit()
+                    for p in takes:
+                        held[p] += 1
+                    for p in frees:
+                        held[p] -= 1
+                    done.add(name)
+                    head[e] += 1
+                    left -= 1
+                    moved = True
+            assert moved, "the orders of the engines block each other"

@@ -18,83 +18,63 @@ P = 128
 E = 1024
 NBLK = 512
 
-KB = (-98.5, -96.5, -93.5)
-BC = ("V", "V", "V")
-VE = {0: (1, 3), 1: (1,)}
-RE = "GGGGGGGG"
-TL = 1.5
-EL = 0.6
-QL = 1.5
-AL = 0.6
-SL = 2.0
-NL = 3.0
-RL = 4.0
-NWARM = 4
-BUFS = {"tp": 4, "acc": 4, "grp": 3}
-
 
 def tile_knnxlmultiheadsattention_pa_kernel(
     tc, x_in, wq, bq, wk, bk, wv, bv, out_q, out_k, out_v
 ):
     nc = tc.nc
     weights = (wq, wk, wv)
-    biases = (bq, bk, bv)
     outs = (out_q, out_k, out_v)
     with ExitStack() as ctx:
         ctx.enter_context(tc.manual_schedule())
         const = ctx.enter_context(tc.tile_pool(name="const", bufs=1))
         raw = ctx.enter_context(tc.tile_pool(name="raw", bufs=1))
-        grp = ctx.enter_context(tc.tile_pool(name="grp", bufs=BUFS["grp"]))
+        grp = ctx.enter_context(tc.tile_pool(name="grp", bufs=3))
         keep = ctx.enter_context(tc.tile_pool(name="keep", bufs=1))
         res = ctx.enter_context(tc.tile_pool(name="res", bufs=1))
         scr = ctx.enter_context(tc.tile_pool(name="scr", bufs=2))
         small = ctx.enter_context(tc.tile_pool(name="small", bufs=1))
-        tpp = ctx.enter_context(tc.psum_pool(name="tpp", bufs=BUFS["tp"]))
-        accp = ctx.enter_context(tc.psum_pool(name="accp", bufs=BUFS["acc"]))
+        tpp = ctx.enter_context(tc.psum_pool(name="tpp", bufs=4))
+        accp = ctx.enter_context(tc.psum_pool(name="accp", bufs=4))
 
         ones = const.tile([P, NBLK], BF16, name="ones")
         nc.gpsimd.memset(ones[:], 1.0)
+        bias_row = const.tile([P, E], BF16, name="bias_row")
+        nc.vector.memset(bias_row[:].bitcast(I32), 0)
+        nc.scalar.dma_start(out=bias_row[0:1, :], in_=bq.rearrange("(o n) -> o n", o=1))
 
-        bzs = []
-        for w in range(3):
-            bz = const.tile([P, E], BF16, name="bz%d" % w)
-            nc.vector.memset(bz[:].bitcast(I32), 0)
-            nc.scalar.dma_start(out=bz[0:1, :], in_=biases[w].rearrange("(o n) -> o n", o=1))
-            bzs.append(bz)
-
-        rows = []
-        xr = []
+        rows = [[]]
         for tt in range(4):
             b, jj = divmod(tt, 2)
             t = raw.tile([P, E], BF16, name="xraw%d" % tt)
             nc.sync.dma_start(out=t[:], in_=x_in[b].rearrange("(p j) e -> p j e", j=2)[:, jj, :])
-            xr.append(t[:])
-        rows.append(xr)
+            rows[0].append(t[:])
         for w in range(3):
             for c in range(2):
                 wsrc = weights[w][c * NBLK : (c + 1) * NBLK, :].rearrange("(p r) k -> p r k", r=4)
-                wr = []
+                rows.append([])
                 for hf in range(2):
                     t = raw.tile([P, 2, E], BF16, name="wraw%d%d%d" % (w, c, hf))
                     nc.sync.dma_start(out=t[:], in_=wsrc[:, 2 * hf : 2 * hf + 2, :])
-                    wr.extend([t[:, 0, :], t[:, 1, :]])
-                rows.append(wr)
+                    rows[-1].extend([t[:, 0, :], t[:, 1, :]])
+        bias = [const.tile([P, E], BF16, name="bias%d" % w) for w in range(3)]
+        for w, src in ((1, bk), (2, bv)):
+            nc.sync.dma_start(out=bias[w][:], in_=src.partition_broadcast(P))
 
         ident = const.tile([P, P], F32, name="ident")
         make_identity(nc, ident[:])
-        mhalf = small.tile([P, 1], F32, name="mhalf")
-        nc.gpsimd.memset(mhalf[:], -0.5)
-        one2 = small.tile([P, 1], F32, name="one2")
-        nc.scalar.activation(out=one2[:], in_=mhalf[:], func=ACT.Square)
+        one = small.tile([P, 1], F32, name="one")
+        nc.gpsimd.memset(one[:], 1.0)
+        root = small.tile([P, 1], F32, name="root")
+        nc.scalar.activation(out=root[:], in_=one[:], func=ACT.Sqrt)
 
-        ops = {}
-        queues = {"PE": [], "V": [], "S": [], "G": [], "SP": []}
-
-        def add(eng, key, name, deps, emit, takes=(), frees=()):
-            ops[name] = (deps, emit, takes, frees)
-            queues[eng].append((key, len(ops), name))
-
-        tiles = {}
+        grouped, codes, planes, tps, accs, pbs = {}, {}, {}, {}, {}, {}
+        y = {}
+        for w in range(3):
+            for b in range(2):
+                y[(w, b)] = res.tile([P, 8, 2, P], F32, name="y%d%d" % (w, b))
+        ss = [small.tile([P, 4, 2], F32, name="ss%d" % w) for w in range(2)]
+        n2, rn = {}, {}
 
         def copy_on(eng, out, in_):
             if eng == "V":
@@ -102,222 +82,185 @@ def tile_knnxlmultiheadsattention_pa_kernel(
             else:
                 nc.scalar.copy(out=out, in_=in_)
 
-        def emit_bmm(w):
-            pb = accp.tile([P, E], BF16, tag="acc", name="pb%d" % w)
-            tiles[("pb", w)] = pb
-            for c in range(2):
-                nc.tensor.matmul(
-                    out=pb[:, c * NBLK : (c + 1) * NBLK],
-                    lhsT=ones[:, 0:P],
-                    rhs=bzs[w][:, c * NBLK : (c + 1) * NBLK],
-                    start=True,
-                    stop=True,
-                )
-
-        def emit_bc(w):
-            bb = const.tile([P, E], BF16, name="bias%d" % w)
-            tiles[("bias", w)] = bb
-            copy_on(BC[w], bb[:], tiles[("pb", w)][:])
-
-        def emit_warm(n):
+        def warm(n):
             pd = accp.tile([P, NBLK], F32, tag="acc", name="warm")
             for k in range(n):
                 nc.tensor.matmul(out=pd[:], lhsT=ones[:, 0:P], rhs=ones[:], start=True, stop=True)
 
-        add("PE", -101.0, "D0", (), lambda: emit_warm(NWARM), takes=("acc",), frees=("acc",))
+        def bmm():
+            pb = accp.tile([P, E], BF16, tag="acc", name="pb")
+            pbs[0] = pb
+            for c in range(2):
+                cols = slice(c * NBLK, (c + 1) * NBLK)
+                nc.tensor.matmul(out=pb[:, cols], lhsT=ones[:, 0:P], rhs=bias_row[:, cols], start=True, stop=True)
 
-        for w in range(3):
-            add("PE", KB[w], "bmm%d" % w, (), lambda w=w: emit_bmm(w), takes=("acc",))
-            add(BC[w], KB[w] + 0.3, "bc%d" % w, ("bmm%d" % w,), lambda w=w: emit_bc(w), frees=("acc",))
+        def bc(eng):
+            copy_on(eng, bias[0][:], pbs[0][:])
 
-        def emit_t(blk, r):
+        def T(blk, r):
             if r == 0:
-                tiles[("g4", blk)] = grp.tile(
-                    [P, 2, NBLK, 4], BF16, tag="g4", name="g4_%d" % blk, align_bytes=64
-                )
+                g4 = grp.tile([P, 2, NBLK, 4], BF16, tag="g4", name="g4_%d" % blk, align_bytes=64)
+                grouped[blk] = g4
             tp = tpp.tile([P, 2, 2, P], F32, tag="tp", name="tp%d_%d" % (blk, r))
-            tiles[("tp", blk, r)] = tp
+            tps[(blk, r)] = tp
             src = rows[blk][r].bitcast(F32)
             for g in range(2):
                 for u in range(2):
-                    nc.tensor.transpose(
-                        tp[:, g, u, :], src[:, 256 * g + u : 256 * (g + 1) : 2], ident[:]
-                    )
+                    nc.tensor.transpose(tp[:, g, u, :], src[:, 256 * g + u : 256 * (g + 1) : 2], ident[:])
 
-        def emit_e(blk, r, eng):
-            gw = tiles[("g4", blk)][:].bitcast(F32)
+        def E_(eng, blk, r):
             copy_on(
                 eng,
-                gw[:, :, r * P : (r + 1) * P, :],
-                tiles[("tp", blk, r)][:].rearrange("p g u r -> p g r u"),
+                grouped[blk][:].bitcast(F32)[:, :, r * P : (r + 1) * P, :],
+                tps[(blk, r)][:].rearrange("p g u r -> p g r u"),
             )
 
-        def emit_q(blk, g):
+        def Q(blk, g):
             if g == 0:
-                tiles[("cd", blk)] = keep.tile([P, 2, NBLK], U32, name="cd%d" % blk, align_bytes=64)
-                tiles[("pl", blk)] = keep.tile([P, 2, NBLK], U8, name="pl%d" % blk, align_bytes=64)
+                cd = keep.tile([P, 2, NBLK], U32, name="cd%d" % blk, align_bytes=64)
+                pl = keep.tile([P, 2, NBLK], U8, name="pl%d" % blk, align_bytes=64)
+                codes[blk], planes[blk] = cd, pl
             nc.vector.quantize_mx(
-                out=tiles[("cd", blk)][:, g, :].bitcast(FP8X4),
-                scales=tiles[("pl", blk)][:, g, :],
-                in_=tiles[("g4", blk)][:, g, :, :].rearrange("p f t -> p (f t)"),
+                out=codes[blk][:, g, :].bitcast(FP8X4),
+                scales=planes[blk][:, g, :],
+                in_=grouped[blk][:, g, :, :].rearrange("p f t -> p (f t)"),
             )
 
-        for blk in range(7):
-            for r in range(4):
-                if blk <= 2:
-                    kt = -100.0 + 4 * blk + r
-                    ke = kt + 0.1
-                else:
-                    j = 4 * (blk - 3) + r
-                    kt = 2 * (j // 2) + 0.01 * (j % 2) + TL
-                    ke = kt + EL
-                eng = "V" if r in VE.get(blk, ()) else "S"
-                add(
-                    "PE", kt, "T%d.%d" % (blk, r), (), lambda blk=blk, r=r: emit_t(blk, r),
-                    takes=("tp", "grp") if r == 0 else ("tp",),
-                )
-                add(
-                    eng, ke, "E%d.%d" % (blk, r), ("T%d.%d" % (blk, r),),
-                    lambda blk=blk, r=r, eng=eng: emit_e(blk, r, eng), frees=("tp",),
-                )
-            for g in range(2):
-                add(
-                    "V", ke + QL + 0.1 * g, "Q%d.%d" % (blk, g), tuple("E%d.%d" % (blk, r) for r in range(4)),
-                    lambda blk=blk, g=g: emit_q(blk, g), frees=("grp",) if g == 1 else (),
-                )
+        def where(i):
+            blk, tt = 1 + i // 4, i % 4
+            w, c = divmod(blk - 1, 2)
+            return blk, tt, w, c
 
-        def emit_m(blk, tt):
-            acc = accp.tile([P, NBLK], F32, tag="acc", name="acc%d_%d" % (blk, tt))
-            tiles[("acc", blk, tt)] = acc
+        def M(i):
+            blk, tt, w, c = where(i)
+            acc = accp.tile([P, NBLK], F32, tag="acc", name="acc%d" % i)
+            accs[i] = acc
             for g in range(2):
                 nc.tensor.matmul_mx(
                     out=acc[:],
-                    lhsT=tiles[("cd", 0)][:, g, tt * P : (tt + 1) * P].bitcast(FP8X4),
-                    lhsT_scale=tiles[("pl", 0)][:, g, tt * P : (tt + 1) * P],
-                    rhs=tiles[("cd", blk)][:, g, :].bitcast(FP8X4),
-                    rhs_scale=tiles[("pl", blk)][:, g, :],
+                    lhsT=codes[0][:, g, tt * P : (tt + 1) * P].bitcast(FP8X4),
+                    lhsT_scale=planes[0][:, g, tt * P : (tt + 1) * P],
+                    rhs=codes[blk][:, g, :].bitcast(FP8X4),
+                    rhs_scale=planes[blk][:, g, :],
                     start=(g == 0),
                     stop=(g == 1),
                 )
 
-        def emit_a(blk, tt):
-            w, c = divmod(blk - 1, 2)
-            b, jj = divmod(tt, 2)
-            if (w, b) not in tiles:
-                tiles[(w, b)] = res.tile([P, 8, 2, P], F32, name="o%d%d" % (w, b))
-            y = tiles[(w, b)][:, 4 * c : 4 * c + 4, jj, :]
+        def tokens(w, c, tt):
+            return y[(w, tt // 2)][:, 4 * c : 4 * c + 4, tt % 2, :]
+
+        def A(i):
+            blk, tt, w, c = where(i)
             nc.vector.tensor_tensor(
-                out=y.rearrange("p h (e r) -> p h e r", r=4),
-                in0=tiles[("acc", blk, tt)][:].rearrange("p (r h e) -> p h e r", r=4, h=4),
-                in1=tiles[("bias", w)][:, c * NBLK : (c + 1) * NBLK].rearrange(
-                    "p (h e r) -> p h e r", h=4, r=4
-                ),
+                out=tokens(w, c, tt).rearrange("p h (e r) -> p h e r", r=4),
+                in0=accs[i][:].rearrange("p (r h e) -> p h e r", r=4, h=4),
+                in1=bias[w][:, c * NBLK : (c + 1) * NBLK].rearrange("p (h e r) -> p h e r", h=4, r=4),
                 op=ALU.add,
             )
 
-        def emit_sq(blk, tt):
-            w, c = divmod(blk - 1, 2)
-            b, jj = divmod(tt, 2)
-            if ("ss", w) not in tiles:
-                tiles[("ss", w)] = small.tile([P, 4, 2], F32, name="ss%d" % w)
-            junk = scr.tile([P, 4, P], F32, tag="junk", name="junk%d_%d" % (blk, tt))
+        def Sq(i):
+            blk, tt, w, c = where(i)
+            junk = scr.tile([P, 4, P], F32, tag="junk", name="junk%d" % i)
             nc.scalar.activation(
-                out=junk[:], in_=tiles[(w, b)][:, 4 * c : 4 * c + 4, jj, :], func=ACT.Square,
-                accum_out=tiles[("ss", w)][:, tt, c : c + 1],
+                out=junk[:], in_=tokens(w, c, tt), func=ACT.Square, accum_out=ss[w][:, tt, c : c + 1]
             )
 
-        def emit_n(w, tt):
-            ss = tiles[("ss", w)]
-            n2 = small.tile([P, 1], F32, name="n2_%d%d" % (w, tt))
-            nc.gpsimd.tensor_tensor(out=n2[:], in0=ss[:, tt, 0:1], in1=ss[:, tt, 1:2], op=ALU.add)
-            m2 = small.tile([P, 1], F32, name="m2_%d%d" % (w, tt))
-            nc.gpsimd.tensor_scalar(out=m2[:], in0=n2[:], scalar1=1e-24, scalar2=None, op0=ALU.max)
-            r2 = small.tile([P, 1], F32, name="r2_%d%d" % (w, tt))
-            tiles[("r2", w, tt)] = r2
-            nc.gpsimd.tensor_tensor(out=r2[:], in0=m2[:], in1=mhalf[:], op=ALU.pow)
+        def N1(w, b):
+            n = small.tile([P, 2], F32, name="n1_%d%d" % (w, b))
+            s = ss[w][:, 2 * b : 2 * b + 2, :]
+            nc.gpsimd.tensor_tensor(out=n[:], in0=s[:, :, 0], in1=s[:, :, 1], op=ALU.add)
+            m = small.tile([P, 2], F32, name="n2_%d%d" % (w, b))
+            nc.gpsimd.tensor_scalar(out=m[:], in0=n[:], scalar1=1e-24, scalar2=None, op0=ALU.max)
+            n2[(w, b)] = m
 
-        def emit_r(w, tt, eng):
-            b, jj = divmod(tt, 2)
-            y = tiles[(w, b)][:, :, jj, :]
-            rr = tiles[("r2", w, tt)][:]
+        def N2(w, b):
+            n = small.tile([P, 2], F32, name="n3_%d%d" % (w, b))
+            nc.scalar.activation(out=n[:], in_=n2[(w, b)][:], func=ACT.Sqrt)
+            n2[(w, b)] = n
+
+        def N3(w, b):
+            n = small.tile([P, 2], F32, name="n4_%d%d" % (w, b))
+            nc.vector.reciprocal(out=n[:], in_=n2[(w, b)][:])
+            rn[(w, b)] = n
+
+        def R(eng, w, tt):
+            v = y[(w, tt // 2)][:, :, tt % 2, :]
+            f = rn[(w, tt // 2)][:, tt % 2 : tt % 2 + 1]
             if eng == "V":
-                nc.vector.tensor_scalar(out=y, in0=y, scalar1=rr, scalar2=None, op0=ALU.mult)
-            elif eng == "G":
-                nc.gpsimd.tensor_scalar(out=y, in0=y, scalar1=rr, scalar2=0.0, op0=ALU.mult, op1=ALU.add)
+                nc.vector.tensor_scalar(out=v, in0=v, scalar1=f, scalar2=None, op0=ALU.mult)
             else:
-                nc.scalar.activation(out=y, in_=y, func=ACT.Copy, scale=rr)
+                nc.scalar.activation(out=v, in_=v, func=ACT.Copy, scale=f)
 
-        def emit_store(w, b, h0, h1):
+        def St(w, b, c):
+            h = slice(4 * c, 4 * c + 4)
             nc.sync.dma_start(
-                out=outs[w][b, h0:h1].rearrange("h (p j) d -> p h (j d)", j=2),
-                in_=tiles[(w, b)][:, h0:h1, :, :].rearrange("p h j d -> p h (j d)"),
+                out=outs[w][b, h].rearrange("h (p j) d -> p h (j d)", j=2),
+                in_=y[(w, b)][:, h, :, :].rearrange("p h j d -> p h (j d)"),
             )
 
-        for i in range(24):
-            blk, tt = 1 + i // 4, i % 4
-            w = (blk - 1) // 2
-            add(
-                "PE", float(i), "M%d.%d" % (blk, tt), ("Q0.0", "Q0.1", "Q%d.0" % blk, "Q%d.1" % blk),
-                lambda blk=blk, tt=tt: emit_m(blk, tt), takes=("acc",),
-            )
-            add(
-                "V", i + AL, "A%d.%d" % (blk, tt), ("M%d.%d" % (blk, tt), "bc%d" % w),
-                lambda blk=blk, tt=tt: emit_a(blk, tt), frees=("acc",),
-            )
-            if w < 2:
-                add(
-                    "S", i + SL, "Sq%d.%d" % (blk, tt), ("A%d.%d" % (blk, tt),),
-                    lambda blk=blk, tt=tt: emit_sq(blk, tt),
-                )
-        for w in range(2):
-            for tt in range(4):
-                i = 8 * w + 4 + tt
-                add(
-                    "G", i + NL, "N%d.%d" % (w, tt), ("Sq%d.%d" % (2 * w + 1, tt), "Sq%d.%d" % (2 * w + 2, tt)),
-                    lambda w=w, tt=tt: emit_n(w, tt),
-                )
-                eng = RE[4 * w + tt]
-                add(
-                    eng, i + RL, "R%d.%d" % (w, tt), ("N%d.%d" % (w, tt),),
-                    lambda w=w, tt=tt, eng=eng: emit_r(w, tt, eng),
-                )
-            for b in range(2):
-                for c in range(2):
-                    add(
-                        "SP", 8 * w + 4 + 2 * b + 6 + 0.1 * c, "St%d%d%d" % (w, b, c),
-                        ("R%d.%d" % (w, 2 * b), "R%d.%d" % (w, 2 * b + 1)),
-                        lambda w=w, b=b, c=c: emit_store(w, b, 4 * c, 4 * c + 4),
-                    )
-        for c in range(2):
-            for b in range(2):
-                add(
-                    "SP", 16.0 + 4 * c + 2 * b + 2.5, "Stv%d%d" % (c, b),
-                    ("A%d.%d" % (5 + c, 2 * b), "A%d.%d" % (5 + c, 2 * b + 1)),
-                    lambda c=c, b=b: emit_store(2, b, 4 * c, 4 * c + 4),
-                )
+        warm(4)
+        for r in range(4):
+            T(0, r)
+            E_("VS"[r % 2 == 0], 0, r)
+        bmm()
+        for r in range(4):
+            T(1, r)
+        Q(0, 0)
+        Q(0, 1)
+        for r in range(4):
+            E_("S", 1, r)
+        bc("V")
+        for r in range(4):
+            T(2, r)
+        Q(1, 0)
+        Q(1, 1)
+        for r in range(4):
+            E_("S", 2, r)
 
-        order = {e: [n for (k, i, n) in sorted(q)] for e, q in queues.items()}
-        head = {e: 0 for e in order}
-        done = set()
-        held = {"tp": 0, "acc": 0, "grp": 0}
-        left = len(ops)
-        while left:
-            moved = False
-            for e in ("PE", "S", "V", "G", "SP"):
-                while head[e] < len(order[e]):
-                    name = order[e][head[e]]
-                    deps, emit, takes, frees = ops[name]
-                    if not all(d in done for d in deps):
-                        break
-                    if not all(held[p] < BUFS[p] for p in takes):
-                        break
-                    emit()
-                    for p in takes:
-                        held[p] += 1
-                    for p in frees:
-                        held[p] -= 1
-                    done.add(name)
-                    head[e] += 1
-                    left -= 1
-                    moved = True
-            assert moved, "the orders of the engines block each other"
+        for b in range(1, 9):
+            i0 = 4 * (b - 1)
+            w = {3: 0, 5: 1}.get(b)
+            if b <= 6:
+                for i in range(i0, i0 + 4):
+                    M(i)
+            if b <= 5:
+                Q(b + 1, 0)
+                Q(b + 1, 1)
+            if b <= 4:
+                for r in range(4):
+                    T(b + 2, r)
+            if b <= 6:
+                A(i0)
+                A(i0 + 1)
+                if b >= 5:
+                    St(2, 0, b - 5)
+            if w is not None:
+                N2(w, 0)
+            if b <= 4:
+                for r in range(4):
+                    E_("S", b + 2, r)
+            if w is not None:
+                N3(w, 0)
+                for j in range(2):
+                    R("VVVVVSVS"[4 * w + j], w, j)
+                St(w, 0, 0)
+                St(w, 0, 1)
+            if b <= 6:
+                A(i0 + 2)
+                A(i0 + 3)
+                if b >= 5:
+                    St(2, 1, b - 5)
+            if w is not None:
+                N2(w, 1)
+            if b <= 4:
+                for i in range(i0, i0 + 4):
+                    Sq(i)
+            if w is not None:
+                N3(w, 1)
+                for j in range(2, 4):
+                    R("VVVVVSVS"[4 * w + j], w, j)
+                St(w, 1, 0)
+                St(w, 1, 1)
+            if b in (2, 4):
+                N1(b // 2 - 1, 0)
+                N1(b // 2 - 1, 1)

@@ -83,7 +83,7 @@ def tile_knnxlmultiheadsattention_pa_kernel(
                 nc.scalar.copy(out=out, in_=in_)
 
         def warm(n):
-            pd = accp.tile([P, NBLK], F32, tag="acc", name="warm")
+            pd = accp.tile([P, NBLK], F32, tag="acc", name="warm%d" % n)
             for k in range(n):
                 nc.tensor.matmul(out=pd[:], lhsT=ones[:, 0:P], rhs=ones[:], start=True, stop=True)
 
@@ -198,69 +198,99 @@ def tile_knnxlmultiheadsattention_pa_kernel(
                 in_=y[(w, b)][:, h, :, :].rearrange("p h j d -> p h (j d)"),
             )
 
-        warm(4)
-        for r in range(4):
-            T(0, r)
-            E_("VS"[r % 2 == 0], 0, r)
-        bmm()
-        for r in range(4):
-            T(1, r)
-        Q(0, 0)
-        Q(0, 1)
-        for r in range(4):
-            E_("S", 1, r)
-        bc("V")
-        for r in range(4):
-            T(2, r)
-        Q(1, 0)
-        Q(1, 1)
-        for r in range(4):
-            E_("S", 2, r)
 
-        for b in range(1, 9):
-            i0 = 4 * (b - 1)
-            w = {3: 0, 5: 1}.get(b)
-            if b <= 6:
-                for i in range(i0, i0 + 4):
-                    M(i)
-            if b <= 5:
-                Q(b + 1, 0)
-                Q(b + 1, 1)
-            if b <= 4:
-                for r in range(4):
-                    T(b + 2, r)
-            if b <= 6:
-                A(i0)
-                A(i0 + 1)
-                if b >= 5:
-                    St(2, 0, b - 5)
-            if w is not None:
-                N2(w, 0)
-            if b <= 4:
-                for r in range(4):
-                    E_("S", b + 2, r)
-            if w is not None:
-                N3(w, 0)
+        pe = [("warm", 8)]
+        after = {(0, 1): ("keep", 0), (1, 3): ("bias", 0)}
+        for blk in range(2):
+            for r in range(4):
+                pe.append(("T", blk, r))
+                if (blk, r) in after:
+                    pe.append(after[(blk, r)])
+        pairs = [(blk, r) for blk in range(2, 7) for r in (0, 2)]
+        for s in range(12):
+            if s < len(pairs):
+                blk, r = pairs[s]
+                pe.extend([("T", blk, r), ("T", blk, r + 1)])
+            pe.extend([("M", 2 * s), ("M", 2 * s + 1)])
+        place = {op: i for i, op in enumerate(pe)}
+
+        ops = {}
+        queues = {"PE": [], "V": [], "S": [], "G": [], "SP": []}
+
+        def add(eng, key, name, deps, emit, takes=(), frees=()):
+            ops[name] = (deps, emit, takes, frees, key)
+            queues[eng].append((key, len(ops), name))
+
+        VE = {0: (1, 3)}
+        RE = "VVVVVVVS"
+        for op in pe:
+            k = float(place[op])
+            if op[0] == "warm":
+                add("PE", k, op, (), lambda n=op[1]: warm(n), takes=("acc",), frees=("acc",))
+            elif op[0] == "keep":
+                add("PE", k, op, (), lambda: warm(2), takes=("acc",), frees=("acc",))
+            elif op[0] == "bias":
+                add("PE", k, op, (), bmm, takes=("acc",))
+                add("S", k + 2.0, ("bc", 0), (op,), lambda: bc("S"), frees=("acc",))
+            elif op[0] == "T":
+                blk, r = op[1:]
+                eng = "V" if r in VE.get(blk, ()) else "S"
+                add("PE", k, op, (), lambda blk=blk, r=r: T(blk, r), takes=("tp", "grp") if r == 0 else ("tp",))
+                add(eng, k + 0.5, ("E", blk, r), (op,), lambda eng=eng, blk=blk, r=r: E_(eng, blk, r), frees=("tp",))
+            else:
+                i = op[1]
+                blk, tt, w, c = where(i)
+                add("PE", k, op, (("Q", 0, 1), ("Q", blk, 1)), lambda i=i: M(i), takes=("acc",))
+                add("V", k + 1.0, ("A", i), (op,) + ((("bc", 0),) if w == 0 else ()), lambda i=i: A(i), frees=("acc",))
+                if w < 2:
+                    add("S", k + 1.0 + 3.0, ("Sq", i), (("A", i),), lambda i=i: Sq(i))
+        for blk in range(7):
+            for g in range(2):
+                add(
+                    "V", max(place[("T", blk, r)] for r in range(4)) + 0.5 + 0.5 + 0.01 * g, ("Q", blk, g),
+                    tuple(("E", blk, r) for r in range(4)), lambda blk=blk, g=g: Q(blk, g), frees=("grp",) if g else (),
+                )
+        for w in range(2):
+            for b in range(2):
+                units = [8 * w + 4 * c + 2 * b + j for c in range(2) for j in range(2)]
+                k = max(ops[("Sq", i)][4] for i in units)
+                add("G", k + 0.5, ("N1", w, b), tuple(("Sq", i) for i in units), lambda w=w, b=b: N1(w, b))
+                add("S", k + 3.0, ("N2", w, b), (("N1", w, b),), lambda w=w, b=b: N2(w, b))
+                add("V", k + 5.0, ("N3", w, b), (("N2", w, b),), lambda w=w, b=b: N3(w, b))
                 for j in range(2):
-                    R("VVVVVSVS"[4 * w + j], w, j)
-                St(w, 0, 0)
-                St(w, 0, 1)
-            if b <= 6:
-                A(i0 + 2)
-                A(i0 + 3)
-                if b >= 5:
-                    St(2, 1, b - 5)
-            if w is not None:
-                N2(w, 1)
-            if b <= 4:
-                for i in range(i0, i0 + 4):
-                    Sq(i)
-            if w is not None:
-                N3(w, 1)
-                for j in range(2, 4):
-                    R("VVVVVSVS"[4 * w + j], w, j)
-                St(w, 1, 0)
-                St(w, 1, 1)
-            if b in (2, 4):
-                N1(b // 2 - 1, 0)
-                N1(b // 2 - 1, 1)
+                    tt = 2 * b + j
+                    eng = RE[4 * w + tt]
+                    add(eng, k + 5.0 + 0.1 + 0.1 * j, ("R", w, tt), (("N3", w, b),), lambda eng=eng, w=w, tt=tt: R(eng, w, tt))
+                for c in range(2):
+                    add("SP", k + 5.0 + 2.0 + 0.1 * c, ("St", w, b, c), (("R", w, 2 * b), ("R", w, 2 * b + 1)), lambda w=w, b=b, c=c: St(w, b, c))
+        for c in range(2):
+            for b in range(2):
+                i = 16 + 4 * c + 2 * b + 1
+                add("SP", ops[("A", i)][4] + 1.0, ("St", 2, b, c), (("A", i - 1), ("A", i)), lambda b=b, c=c: St(2, b, c))
+
+        order = {e: [n for (k, i, n) in sorted(q)] for e, q in queues.items()}
+        head = {e: 0 for e in order}
+        done = set()
+        bufs = {"tp": 4, "acc": 4, "grp": 3}
+        held = {"tp": 0, "acc": 0, "grp": 0}
+        left = len(ops)
+        while left:
+            moved = False
+            for e in ("PE", "S", "V", "G", "SP"):
+                while head[e] < len(order[e]):
+                    name = order[e][head[e]]
+                    deps, emit, takes, frees, key = ops[name]
+                    if not all(d in done for d in deps):
+                        break
+                    if not all(held[p] < bufs[p] for p in takes):
+                        break
+                    emit()
+                    for p in takes:
+                        held[p] += 1
+                    for p in frees:
+                        held[p] -= 1
+                    done.add(name)
+                    head[e] += 1
+                    left -= 1
+                    moved = True
+            assert moved, "the orders of the engines block each other"

@@ -39,9 +39,12 @@ def tile_knnxlmultiheadsattention_pa_kernel(
 
         ones = const.tile([P, NBLK], BF16, name="ones")
         nc.gpsimd.memset(ones[:], 1.0)
-        bias_row = const.tile([P, E], BF16, name="bias_row")
-        nc.vector.memset(bias_row[:].bitcast(I32), 0)
-        nc.scalar.dma_start(out=bias_row[0:1, :], in_=bq.rearrange("(o n) -> o n", o=1))
+        bias_rows = []
+        for w, src in enumerate((bq, bk, bv)):
+            row = const.tile([P, E], BF16, name="bias_row%d" % w)
+            nc.vector.memset(row[:].bitcast(I32), 0)
+            nc.scalar.dma_start(out=row[0:1, :], in_=src.rearrange("(o n) -> o n", o=1))
+            bias_rows.append(row)
 
         rows = [[]]
         for tt in range(4):
@@ -58,8 +61,6 @@ def tile_knnxlmultiheadsattention_pa_kernel(
                     nc.sync.dma_start(out=t[:], in_=wsrc[:, 2 * hf : 2 * hf + 2, :])
                     rows[-1].extend([t[:, 0, :], t[:, 1, :]])
         bias = [const.tile([P, E], BF16, name="bias%d" % w) for w in range(3)]
-        for w, src in ((1, bk), (2, bv)):
-            nc.sync.dma_start(out=bias[w][:], in_=src.partition_broadcast(P))
 
         ident = const.tile([P, P], F32, name="ident")
         make_identity(nc, ident[:])
@@ -87,15 +88,15 @@ def tile_knnxlmultiheadsattention_pa_kernel(
             for k in range(n):
                 nc.tensor.matmul(out=pd[:], lhsT=ones[:, 0:P], rhs=ones[:], start=True, stop=True)
 
-        def bmm():
-            pb = accp.tile([P, E], BF16, tag="acc", name="pb")
-            pbs[0] = pb
+        def bmm(w):
+            pb = accp.tile([P, E], BF16, tag="acc", name="pb%d" % w)
+            pbs[w] = pb
             for c in range(2):
                 cols = slice(c * NBLK, (c + 1) * NBLK)
-                nc.tensor.matmul(out=pb[:, cols], lhsT=ones[:, 0:P], rhs=bias_row[:, cols], start=True, stop=True)
+                nc.tensor.matmul(out=pb[:, cols], lhsT=ones[:, 0:P], rhs=bias_rows[w][:, cols], start=True, stop=True)
 
-        def bc(eng):
-            copy_on(eng, bias[0][:], pbs[0][:])
+        def bc(eng, w):
+            copy_on(eng, bias[w][:], pbs[w][:])
 
         def T(blk, r):
             if r == 0:
@@ -200,7 +201,7 @@ def tile_knnxlmultiheadsattention_pa_kernel(
 
 
         pe = [("warm", 8)]
-        after = {(0, 1): ("keep", 0), (1, 3): ("bias", 0)}
+        after = {(1, 1): ("bias", 0), (1, 3): ("bias", 1), (2, 1): ("bias", 2)}
         for blk in range(2):
             for r in range(4):
                 pe.append(("T", blk, r))
@@ -211,6 +212,8 @@ def tile_knnxlmultiheadsattention_pa_kernel(
             if s < len(pairs):
                 blk, r = pairs[s]
                 pe.extend([("T", blk, r), ("T", blk, r + 1)])
+                if (blk, r + 1) in after:
+                    pe.append(after[(blk, r + 1)])
             pe.extend([("M", 2 * s), ("M", 2 * s + 1)])
         place = {op: i for i, op in enumerate(pe)}
 
@@ -222,6 +225,7 @@ def tile_knnxlmultiheadsattention_pa_kernel(
             queues[eng].append((key, len(ops), name))
 
         VE = {0: (1, 3)}
+        BC = "SVS"
         RE = "VVVVVVVS"
         for op in pe:
             k = float(place[op])
@@ -230,8 +234,9 @@ def tile_knnxlmultiheadsattention_pa_kernel(
             elif op[0] == "keep":
                 add("PE", k, op, (), lambda: warm(2), takes=("acc",), frees=("acc",))
             elif op[0] == "bias":
-                add("PE", k, op, (), bmm, takes=("acc",))
-                add("S", k + 2.0, ("bc", 0), (op,), lambda: bc("S"), frees=("acc",))
+                w, eng = op[1], BC[op[1]]
+                add("PE", k, op, (), lambda w=w: bmm(w), takes=("acc",))
+                add(eng, k + 1.0, ("bc", w), (op,), lambda eng=eng, w=w: bc(eng, w), frees=("acc",))
             elif op[0] == "T":
                 blk, r = op[1:]
                 eng = "V" if r in VE.get(blk, ()) else "S"
@@ -241,7 +246,7 @@ def tile_knnxlmultiheadsattention_pa_kernel(
                 i = op[1]
                 blk, tt, w, c = where(i)
                 add("PE", k, op, (("Q", 0, 1), ("Q", blk, 1)), lambda i=i: M(i), takes=("acc",))
-                add("V", k + 1.0, ("A", i), (op,) + ((("bc", 0),) if w == 0 else ()), lambda i=i: A(i), frees=("acc",))
+                add("V", k + 1.0, ("A", i), (op, ("bc", w)), lambda i=i: A(i), frees=("acc",))
                 if w < 2:
                     add("S", k + 1.0 + 3.0, ("Sq", i), (("A", i),), lambda i=i: Sq(i))
         for blk in range(7):

@@ -70,6 +70,7 @@ def tile_knnxlmultiheadsattention_pa_kernel(
         nc.scalar.activation(out=root[:], in_=one[:], func=ACT.Sqrt)
 
         grouped, codes, planes, tps, accs, pbs = {}, {}, {}, {}, {}, {}
+        warms = []
         y = {}
         for w in range(3):
             for b in range(2):
@@ -84,7 +85,8 @@ def tile_knnxlmultiheadsattention_pa_kernel(
                 nc.scalar.copy(out=out, in_=in_)
 
         def warm(n):
-            pd = accp.tile([P, NBLK], F32, tag="acc", name="warm%d" % n)
+            pd = accp.tile([P, NBLK], F32, tag="acc", name="warm%d" % len(warms))
+            warms.append(pd)
             for k in range(n):
                 nc.tensor.matmul(out=pd[:], lhsT=ones[:, 0:P], rhs=ones[:], start=True, stop=True)
 
@@ -167,11 +169,13 @@ def tile_knnxlmultiheadsattention_pa_kernel(
             )
 
         def N1(w, b):
-            n = small.tile([P, 2], F32, name="n1_%d%d" % (w, b))
-            s = ss[w][:, 2 * b : 2 * b + 2, :]
-            nc.gpsimd.tensor_tensor(out=n[:], in0=s[:, :, 0], in1=s[:, :, 1], op=ALU.add)
             m = small.tile([P, 2], F32, name="n2_%d%d" % (w, b))
-            nc.gpsimd.tensor_scalar(out=m[:], in0=n[:], scalar1=1e-24, scalar2=None, op0=ALU.max)
+            for j in range(2):
+                tt = 2 * b + j
+                nc.vector.tensor_scalar(
+                    out=m[:, j : j + 1], in0=ss[w][:, tt, 0:1], scalar1=ss[w][:, tt, 1:2], scalar2=1e-24,
+                    op0=ALU.add, op1=ALU.max,
+                )
             n2[(w, b)] = m
 
         def N2(w, b):
@@ -200,8 +204,8 @@ def tile_knnxlmultiheadsattention_pa_kernel(
             )
 
 
-        pe = [("warm", 8)]
-        after = {(1, 1): ("bias", 0), (1, 3): ("bias", 1), (2, 1): ("bias", 2)}
+        pe = [("warm", 4)]
+        after = {(0, 1): ("keep", 0), (0, 3): ("keep", 1), (1, 1): ("bias", 0), (1, 3): ("bias", 1), (2, 1): ("bias", 2)}
         for blk in range(2):
             for r in range(4):
                 pe.append(("T", blk, r))
@@ -218,7 +222,7 @@ def tile_knnxlmultiheadsattention_pa_kernel(
         place = {op: i for i, op in enumerate(pe)}
 
         ops = {}
-        queues = {"PE": [], "V": [], "S": [], "G": [], "SP": []}
+        queues = {"PE": [], "V": [], "S": [], "SP": []}
 
         def add(eng, key, name, deps, emit, takes=(), frees=()):
             ops[name] = (deps, emit, takes, frees, key)
@@ -259,7 +263,7 @@ def tile_knnxlmultiheadsattention_pa_kernel(
             for b in range(2):
                 units = [8 * w + 4 * c + 2 * b + j for c in range(2) for j in range(2)]
                 k = max(ops[("Sq", i)][4] for i in units)
-                add("G", k + 0.5, ("N1", w, b), tuple(("Sq", i) for i in units), lambda w=w, b=b: N1(w, b))
+                add("V", k + 1.0, ("N1", w, b), tuple(("Sq", i) for i in units), lambda w=w, b=b: N1(w, b))
                 add("S", k + 3.0, ("N2", w, b), (("N1", w, b),), lambda w=w, b=b: N2(w, b))
                 add("V", k + 5.0, ("N3", w, b), (("N2", w, b),), lambda w=w, b=b: N3(w, b))
                 for j in range(2):
@@ -281,7 +285,7 @@ def tile_knnxlmultiheadsattention_pa_kernel(
         left = len(ops)
         while left:
             moved = False
-            for e in ("PE", "S", "V", "G", "SP"):
+            for e in ("PE", "S", "V", "SP"):
                 while head[e] < len(order[e]):
                     name = order[e][head[e]]
                     deps, emit, takes, frees, key = ops[name]

@@ -75,7 +75,7 @@ def tile_knnxlmultiheadsattention_pa_kernel(
         for w in range(3):
             for b in range(2):
                 y[(w, b)] = res.tile([P, 8, 2, P], F32, name="y%d%d" % (w, b))
-        ss = [small.tile([P, 4, 2], F32, name="ss%d" % w) for w in range(2)]
+        ss = [small.tile([P, 4], F32, name="ss%d" % w) for w in range(2)]
         n2, rn = {}, {}
 
         def copy_on(eng, out, in_):
@@ -129,15 +129,9 @@ def tile_knnxlmultiheadsattention_pa_kernel(
                 in_=grouped[blk][:, g, :, :].rearrange("p f t -> p (f t)"),
             )
 
-        def where(i):
-            blk, tt = 1 + i // 4, i % 4
-            w, c = divmod(blk - 1, 2)
-            return blk, tt, w, c
-
-        def M(i):
-            blk, tt, w, c = where(i)
-            acc = accp.tile([P, NBLK], F32, tag="acc", name="acc%d" % i)
-            accs[i] = acc
+        def M(blk, tt):
+            acc = accp.tile([P, NBLK], F32, tag="acc", name="acc%d_%d" % (blk, tt))
+            accs[(blk, tt)] = acc
             for g in range(2):
                 nc.tensor.matmul_mx(
                     out=acc[:],
@@ -149,33 +143,26 @@ def tile_knnxlmultiheadsattention_pa_kernel(
                     stop=(g == 1),
                 )
 
-        def tokens(w, c, tt):
-            return y[(w, tt // 2)][:, 4 * c : 4 * c + 4, tt % 2, :]
-
-        def A(i):
-            blk, tt, w, c = where(i)
+        def A(blk, tt, h0=0, h1=4):
+            w, c = divmod(blk - 1, 2)
             nc.vector.tensor_tensor(
-                out=tokens(w, c, tt).rearrange("p h (e r) -> p h e r", r=4),
-                in0=accs[i][:].rearrange("p (r h e) -> p h e r", r=4, h=4),
-                in1=bias[w][:, c * NBLK : (c + 1) * NBLK].rearrange("p (h e r) -> p h e r", h=4, r=4),
+                out=y[(w, tt // 2)][:, 4 * c + h0 : 4 * c + h1, tt % 2, :].rearrange("p h (e r) -> p h e r", r=4),
+                in0=accs[(blk, tt)][:].rearrange("p (r h e) -> p h e r", r=4, h=4)[:, h0:h1, :, :],
+                in1=bias[w][:, c * NBLK : (c + 1) * NBLK].rearrange("p (h e r) -> p h e r", h=4, r=4)[:, h0:h1, :, :],
                 op=ALU.add,
             )
 
-        def Sq(i):
-            blk, tt, w, c = where(i)
-            junk = scr.tile([P, 4, P], F32, tag="junk", name="junk%d" % i)
+        def Sq(w, tt):
+            junk = scr.tile([P, 8, P], F32, tag="junk", name="junk%d_%d" % (w, tt))
             nc.scalar.activation(
-                out=junk[:], in_=tokens(w, c, tt), func=ACT.Square, accum_out=ss[w][:, tt, c : c + 1]
+                out=junk[:], in_=y[(w, tt // 2)][:, :, tt % 2, :], func=ACT.Square, accum_out=ss[w][:, tt : tt + 1]
             )
 
         def N1(w, b):
             m = small.tile([P, 2], F32, name="n2_%d%d" % (w, b))
-            for j in range(2):
-                tt = 2 * b + j
-                nc.vector.tensor_scalar(
-                    out=m[:, j : j + 1], in0=ss[w][:, tt, 0:1], scalar1=ss[w][:, tt, 1:2], scalar2=1e-24,
-                    op0=ALU.add, op1=ALU.max,
-                )
+            nc.vector.tensor_scalar(
+                out=m[:], in0=ss[w][:, 2 * b : 2 * b + 2], scalar1=1e-24, scalar2=None, op0=ALU.max
+            )
             n2[(w, b)] = m
 
         def N2(w, b):
@@ -196,29 +183,40 @@ def tile_knnxlmultiheadsattention_pa_kernel(
             else:
                 nc.scalar.activation(out=v, in_=v, func=ACT.Copy, scale=f)
 
-        def St(w, b, c):
-            h = slice(4 * c, 4 * c + 4)
+        def St(w, b, h0, h1):
+            h = slice(h0, h1)
             nc.sync.dma_start(
                 out=outs[w][b, h].rearrange("h (p j) d -> p h (j d)", j=2),
                 in_=y[(w, b)][:, h, :, :].rearrange("p h j d -> p h (j d)"),
             )
 
 
-        pe = [("warm", 4)]
-        after = {(0, 1): ("keep", 0), (0, 3): ("keep", 1), (1, 1): ("bias", 0), (1, 3): ("bias", 1), (2, 1): ("bias", 2)}
-        for blk in range(2):
-            for r in range(4):
-                pe.append(("T", blk, r))
-                if (blk, r) in after:
-                    pe.append(after[(blk, r)])
-        pairs = [(blk, r) for blk in range(2, 7) for r in (0, 2)]
-        for s in range(12):
-            if s < len(pairs):
+        after = {
+            ("T", 0, 1): ("keep",),
+            ("T", 0, 3): ("bias", 0),
+            ("T", 1, 1): ("bias", 1),
+            ("T", 1, 3): ("bias", 2),
+        }
+        units = [(2 * w + 1 + c, 2 * b + j) for w in range(2) for b in range(2) for c in range(2) for j in range(2)]
+        units += [(5 + c, 2 * b + j) for c in range(2) for b in range(2) for j in range(2)]
+        pe = [("warm",)]
+
+        def push(op):
+            pe.append(op)
+            if op in after:
+                pe.append(after[op])
+
+        for r in range(4):
+            push(("T", 0, r))
+        pairs = [(blk, r) for blk in range(1, 7) for r in (0, 2)]
+        for s in range(12 + 4):
+            if s < 12:
                 blk, r = pairs[s]
-                pe.extend([("T", blk, r), ("T", blk, r + 1)])
-                if (blk, r + 1) in after:
-                    pe.append(after[(blk, r + 1)])
-            pe.extend([("M", 2 * s), ("M", 2 * s + 1)])
+                push(("T", blk, r))
+                push(("T", blk, r + 1))
+            if s >= 4:
+                for blk, tt in units[2 * (s - 4) : 2 * (s - 4) + 2]:
+                    push(("M", blk, tt))
         place = {op: i for i, op in enumerate(pe)}
 
         ops = {}
@@ -228,13 +226,13 @@ def tile_knnxlmultiheadsattention_pa_kernel(
             ops[name] = (deps, emit, takes, frees, key)
             queues[eng].append((key, len(ops), name))
 
-        VE = {0: (1, 3)}
-        BC = "SVS"
+        VE = ((0, 1), (0, 3))
+        BC = "SVV"
         RE = "VVVVVVVS"
         for op in pe:
             k = float(place[op])
             if op[0] == "warm":
-                add("PE", k, op, (), lambda n=op[1]: warm(n), takes=("acc",), frees=("acc",))
+                add("PE", k, op, (), lambda: warm(4), takes=("acc",), frees=("acc",))
             elif op[0] == "keep":
                 add("PE", k, op, (), lambda: warm(2), takes=("acc",), frees=("acc",))
             elif op[0] == "bias":
@@ -243,39 +241,51 @@ def tile_knnxlmultiheadsattention_pa_kernel(
                 add(eng, k + 1.0, ("bc", w), (op,), lambda eng=eng, w=w: bc(eng, w), frees=("acc",))
             elif op[0] == "T":
                 blk, r = op[1:]
-                eng = "V" if r in VE.get(blk, ()) else "S"
+                eng = "V" if (blk, r) in VE else "S"
                 add("PE", k, op, (), lambda blk=blk, r=r: T(blk, r), takes=("tp", "grp") if r == 0 else ("tp",))
-                add(eng, k + 0.5, ("E", blk, r), (op,), lambda eng=eng, blk=blk, r=r: E_(eng, blk, r), frees=("tp",))
+                add(eng, k + 2.0, ("E", blk, r), (op,), lambda eng=eng, blk=blk, r=r: E_(eng, blk, r), frees=("tp",))
             else:
-                i = op[1]
-                blk, tt, w, c = where(i)
-                add("PE", k, op, (("Q", 0, 1), ("Q", blk, 1)), lambda i=i: M(i), takes=("acc",))
-                add("V", k + 1.0, ("A", i), (op, ("bc", w)), lambda i=i: A(i), frees=("acc",))
-                if w < 2:
-                    add("S", k + 1.0 + 3.0, ("Sq", i), (("A", i),), lambda i=i: Sq(i))
+                blk, tt = op[1:]
+                w = (blk - 1) // 2
+                add("PE", k, op, (("Q", 0, 1), ("Q", blk, 1)), lambda blk=blk, tt=tt: M(blk, tt), takes=("acc",))
+                if (blk, tt) in units[-2:]:
+                    for q in range(2):
+                        add(
+                            "V", place[("M",) + units[-1]] + 0.5 + 0.2 * q, ("A", blk, tt, q), (op, ("bc", w)),
+                            lambda blk=blk, tt=tt, q=q: A(blk, tt, 2 * q, 2 * q + 2), frees=("acc",) if q else (),
+                        )
+                else:
+                    add("V", k + 0.5, ("A", blk, tt), (op, ("bc", w)), lambda blk=blk, tt=tt: A(blk, tt), frees=("acc",))
         for blk in range(7):
             for g in range(2):
                 add(
-                    "V", max(place[("T", blk, r)] for r in range(4)) + 0.5 + 0.5 + 0.01 * g, ("Q", blk, g),
+                    "V", max(place[("T", blk, r)] for r in range(4)) + 2.0 + 1.0 + 0.01 * g, ("Q", blk, g),
                     tuple(("E", blk, r) for r in range(4)), lambda blk=blk, g=g: Q(blk, g), frees=("grp",) if g else (),
                 )
         for w in range(2):
             for b in range(2):
-                units = [8 * w + 4 * c + 2 * b + j for c in range(2) for j in range(2)]
-                k = max(ops[("Sq", i)][4] for i in units)
-                add("V", k + 1.0, ("N1", w, b), tuple(("Sq", i) for i in units), lambda w=w, b=b: N1(w, b))
-                add("S", k + 3.0, ("N2", w, b), (("N1", w, b),), lambda w=w, b=b: N2(w, b))
+                for tt in (2 * b, 2 * b + 1):
+                    srcs = (("A", 2 * w + 1, tt), ("A", 2 * w + 2, tt))
+                    add("S", max(ops[s][4] for s in srcs) + 1.5, ("Sq", w, tt), srcs, lambda w=w, tt=tt: Sq(w, tt))
+                k = ops[("Sq", w, 2 * b + 1)][4]
+                add("V", k + 1.5, ("N1", w, b), (("Sq", w, 2 * b), ("Sq", w, 2 * b + 1)), lambda w=w, b=b: N1(w, b))
+                add("S", k + 1.5, ("N2", w, b), (("N1", w, b),), lambda w=w, b=b: N2(w, b))
                 add("V", k + 5.0, ("N3", w, b), (("N2", w, b),), lambda w=w, b=b: N3(w, b))
                 for j in range(2):
                     tt = 2 * b + j
                     eng = RE[4 * w + tt]
-                    add(eng, k + 5.0 + 0.1 + 0.1 * j, ("R", w, tt), (("N3", w, b),), lambda eng=eng, w=w, tt=tt: R(eng, w, tt))
+                    add(eng, k + 5.0 + 0.1 + 1.0 * j, ("R", w, tt), (("N3", w, b),), lambda eng=eng, w=w, tt=tt: R(eng, w, tt))
                 for c in range(2):
-                    add("SP", k + 5.0 + 2.0 + 0.1 * c, ("St", w, b, c), (("R", w, 2 * b), ("R", w, 2 * b + 1)), lambda w=w, b=b, c=c: St(w, b, c))
+                    add("SP", k + 5.0 + 2.0 + 0.1 * c, ("St", w, b, c), (("R", w, 2 * b), ("R", w, 2 * b + 1)), lambda w=w, b=b, c=c: St(w, b, 4 * c, 4 * c + 4))
         for c in range(2):
             for b in range(2):
-                i = 16 + 4 * c + 2 * b + 1
-                add("SP", ops[("A", i)][4] + 1.0, ("St", 2, b, c), (("A", i - 1), ("A", i)), lambda b=b, c=c: St(2, b, c))
+                if (5 + c, 2 * b + 1) == units[-1]:
+                    for q in range(2):
+                        srcs = (("A", 5 + c, 2 * b, q), ("A", 5 + c, 2 * b + 1, q))
+                        add("SP", ops[srcs[1]][4] + 1.0, ("St", 2, b, c, q), srcs, lambda b=b, c=c, q=q: St(2, b, 4 * c + 2 * q, 4 * c + 2 * q + 2))
+                else:
+                    srcs = (("A", 5 + c, 2 * b), ("A", 5 + c, 2 * b + 1))
+                    add("SP", ops[srcs[1]][4] + 1.0, ("St", 2, b, c), srcs, lambda b=b, c=c: St(2, b, 4 * c, 4 * c + 4))
 
         order = {e: [n for (k, i, n) in sorted(q)] for e, q in queues.items()}
         head = {e: 0 for e in order}

@@ -191,32 +191,16 @@ def tile_knnxlmultiheadsattention_pa_kernel(
             )
 
 
-        after = {
-            ("T", 0, 1): ("keep",),
-            ("T", 0, 3): ("bias", 0),
-            ("T", 1, 1): ("bias", 1),
-            ("T", 1, 3): ("bias", 2),
-        }
         units = [(2 * w + 1 + c, 2 * b + j) for w in range(2) for b in range(2) for c in range(2) for j in range(2)]
         units += [(5 + c, 2 * b + j) for c in range(2) for b in range(2) for j in range(2)]
         pe = [("warm",)]
-
-        def push(op):
-            pe.append(op)
-            if op in after:
-                pe.append(after[op])
-
-        for r in range(4):
-            push(("T", 0, r))
-        pairs = [(blk, r) for blk in range(1, 7) for r in (0, 2)]
-        for s in range(12 + 4):
-            if s < 12:
-                blk, r = pairs[s]
-                push(("T", blk, r))
-                push(("T", blk, r + 1))
-            if s >= 4:
-                for blk, tt in units[2 * (s - 4) : 2 * (s - 4) + 2]:
-                    push(("M", blk, tt))
+        for blk in range(7):
+            pe.extend([("T", blk, r) for r in range(4)])
+            if blk < 3:
+                pe.append(("bias", blk))
+            else:
+                pe.extend([("M",) + u for u in units[4 * (blk - 3) : 4 * (blk - 3) + 4]])
+        pe.extend([("M",) + u for u in units[16:]])
         place = {op: i for i, op in enumerate(pe)}
 
         ops = {}
@@ -227,23 +211,21 @@ def tile_knnxlmultiheadsattention_pa_kernel(
             queues[eng].append((key, len(ops), name))
 
         VE = ((0, 1), (0, 3))
-        BC = "SVV"
-        RE = "VVVVVVVS"
+        BC = "VVV"
+        RE = "VVVVVSVS"
         for op in pe:
             k = float(place[op])
             if op[0] == "warm":
                 add("PE", k, op, (), lambda: warm(4), takes=("acc",), frees=("acc",))
-            elif op[0] == "keep":
-                add("PE", k, op, (), lambda: warm(2), takes=("acc",), frees=("acc",))
             elif op[0] == "bias":
                 w, eng = op[1], BC[op[1]]
                 add("PE", k, op, (), lambda w=w: bmm(w), takes=("acc",))
-                add(eng, k + 1.0, ("bc", w), (op,), lambda eng=eng, w=w: bc(eng, w), frees=("acc",))
+                add(eng, k + 3.0, ("bc", w), (op,), lambda eng=eng, w=w: bc(eng, w), frees=("acc",))
             elif op[0] == "T":
                 blk, r = op[1:]
                 eng = "V" if (blk, r) in VE else "S"
                 add("PE", k, op, (), lambda blk=blk, r=r: T(blk, r), takes=("tp", "grp") if r == 0 else ("tp",))
-                add(eng, k + 2.0, ("E", blk, r), (op,), lambda eng=eng, blk=blk, r=r: E_(eng, blk, r), frees=("tp",))
+                add(eng, k + 3.0, ("E", blk, r), (op,), lambda eng=eng, blk=blk, r=r: E_(eng, blk, r), frees=("tp",))
             else:
                 blk, tt = op[1:]
                 w = (blk - 1) // 2
@@ -259,24 +241,24 @@ def tile_knnxlmultiheadsattention_pa_kernel(
         for blk in range(7):
             for g in range(2):
                 add(
-                    "V", max(place[("T", blk, r)] for r in range(4)) + 2.0 + 1.0 + 0.01 * g, ("Q", blk, g),
+                    "V", max(place[("T", blk, r)] for r in range(4)) + 3.0 + 1.5 + 0.01 * g, ("Q", blk, g),
                     tuple(("E", blk, r) for r in range(4)), lambda blk=blk, g=g: Q(blk, g), frees=("grp",) if g else (),
                 )
         for w in range(2):
             for b in range(2):
                 for tt in (2 * b, 2 * b + 1):
                     srcs = (("A", 2 * w + 1, tt), ("A", 2 * w + 2, tt))
-                    add("S", max(ops[s][4] for s in srcs) + 1.5, ("Sq", w, tt), srcs, lambda w=w, tt=tt: Sq(w, tt))
+                    add("S", max(ops[s][4] for s in srcs) + 2.0, ("Sq", w, tt), srcs, lambda w=w, tt=tt: Sq(w, tt))
                 k = ops[("Sq", w, 2 * b + 1)][4]
-                add("V", k + 1.5, ("N1", w, b), (("Sq", w, 2 * b), ("Sq", w, 2 * b + 1)), lambda w=w, b=b: N1(w, b))
-                add("S", k + 1.5, ("N2", w, b), (("N1", w, b),), lambda w=w, b=b: N2(w, b))
+                add("V", k + 3.0, ("N1", w, b), (("Sq", w, 2 * b), ("Sq", w, 2 * b + 1)), lambda w=w, b=b: N1(w, b))
+                add("S", k + 3.0, ("N2", w, b), (("N1", w, b),), lambda w=w, b=b: N2(w, b))
                 add("V", k + 5.0, ("N3", w, b), (("N2", w, b),), lambda w=w, b=b: N3(w, b))
                 for j in range(2):
                     tt = 2 * b + j
                     eng = RE[4 * w + tt]
                     add(eng, k + 5.0 + 0.1 + 1.0 * j, ("R", w, tt), (("N3", w, b),), lambda eng=eng, w=w, tt=tt: R(eng, w, tt))
                 for c in range(2):
-                    add("SP", k + 5.0 + 2.0 + 0.1 * c, ("St", w, b, c), (("R", w, 2 * b), ("R", w, 2 * b + 1)), lambda w=w, b=b, c=c: St(w, b, 4 * c, 4 * c + 4))
+                    add("SP", k + 5.0 + 3.0 + 0.1 * c, ("St", w, b, c), (("R", w, 2 * b), ("R", w, 2 * b + 1)), lambda w=w, b=b, c=c: St(w, b, 4 * c, 4 * c + 4))
         for c in range(2):
             for b in range(2):
                 if (5 + c, 2 * b + 1) == units[-1]:

from contextlib import ExitStack

import concourse.mybir as mybir
from concourse.masks import make_identity

FLOPS = 2 * 512 * 1024 * 3072

FP8X4 = mybir.dt.float8_e4m3fn_x4
F32 = mybir.dt.float32
BF16 = mybir.dt.bfloat16
U32 = mybir.dt.uint32
U8 = mybir.dt.uint8
I32 = mybir.dt.int32
ALU = mybir.AluOpType
ACT = mybir.ActivationFunctionType

P = 128
E = 1024
NBLK = 512


def tile_knnxlmultiheadsattention_pa_kernel(
    tc, x_in, wq, bq, wk, bk, wv, bv, out_q, out_k, out_v
):
    nc = tc.nc
    weights = (wq, wk, wv)
    outs = (out_q, out_k, out_v)
    with ExitStack() as ctx:
        ctx.enter_context(tc.manual_schedule())
        const = ctx.enter_context(tc.tile_pool(name="const", bufs=1))
        raw = ctx.enter_context(tc.tile_pool(name="raw", bufs=1))
        grp = ctx.enter_context(tc.tile_pool(name="grp", bufs=3))
        keep = ctx.enter_context(tc.tile_pool(name="keep", bufs=1))
        res = ctx.enter_context(tc.tile_pool(name="res", bufs=1))
        scr = ctx.enter_context(tc.tile_pool(name="scr", bufs=2))
        small = ctx.enter_context(tc.tile_pool(name="small", bufs=1))
        tpp = ctx.enter_context(tc.psum_pool(name="tpp", bufs=4))
        accp = ctx.enter_context(tc.psum_pool(name="accp", bufs=4))

        ones = const.tile([P, NBLK], BF16, name="ones")
        nc.gpsimd.memset(ones[:], 1.0)
        bias_rows = []
        for w, src in enumerate((bq, bk, bv)):
            row = const.tile([P, E], BF16, name="bias_row%d" % w)
            nc.vector.memset(row[:].bitcast(I32), 0)
            nc.scalar.dma_start(out=row[0:1, :], in_=src.rearrange("(o n) -> o n", o=1))
            bias_rows.append(row)

        rows = [[]]
        for tt in range(4):
            b, jj = divmod(tt, 2)
            t = raw.tile([P, E], BF16, name="xraw%d" % tt)
            nc.sync.dma_start(out=t[:], in_=x_in[b].rearrange("(p j) e -> p j e", j=2)[:, jj, :])
            rows[0].append(t[:])
        for w in range(3):
            for c in range(2):
                wsrc = weights[w][c * NBLK : (c + 1) * NBLK, :].rearrange("(p r) k -> p r k", r=4)
                rows.append([])
                for hf in range(2):
                    t = raw.tile([P, 2, E], BF16, name="wraw%d%d%d" % (w, c, hf))
                    nc.sync.dma_start(out=t[:], in_=wsrc[:, 2 * hf : 2 * hf + 2, :])
                    rows[-1].extend([t[:, 0, :], t[:, 1, :]])
        bias = [const.tile([P, E], BF16, name="bias%d" % w) for w in range(3)]

        ident = const.tile([P, P], F32, name="ident")
        make_identity(nc, ident[:])
        one = small.tile([P, 1], F32, name="one")
        nc.gpsimd.memset(one[:], 1.0)
        root = small.tile([P, 1], F32, name="root")
        nc.scalar.activation(out=root[:], in_=one[:], func=ACT.Sqrt)

        grouped, codes, planes, tps, accs, pbs = {}, {}, {}, {}, {}, {}
        warms = []
        y = {}
        for w in range(3):
            for b in range(2):
                y[(w, b)] = res.tile([P, 8, 2, P], F32, name="y%d%d" % (w, b))
        ss = [small.tile([P, 4], F32, name="ss%d" % w) for w in range(2)]
        n2, rn = {}, {}

        def copy_on(eng, out, in_):
            if eng == "V":
                nc.vector.tensor_copy(out=out, in_=in_)
            else:
                nc.scalar.copy(out=out, in_=in_)

        def warm(n):
            pd = accp.tile([P, NBLK], F32, tag="acc", name="warm%d" % len(warms))
            warms.append(pd)
            for k in range(n):
                nc.tensor.matmul(out=pd[:], lhsT=ones[:, 0:P], rhs=ones[:], start=True, stop=True)

        def bmm(w):
            pb = accp.tile([P, E], BF16, tag="acc", name="pb%d" % w)
            pbs[w] = pb
            for c in range(2):
                cols = slice(c * NBLK, (c + 1) * NBLK)
                nc.tensor.matmul(out=pb[:, cols], lhsT=ones[:, 0:P], rhs=bias_rows[w][:, cols], start=True, stop=True)

        def bc(eng, w):
            copy_on(eng, bias[w][:], pbs[w][:])

        def T(blk, r):
            if r == 0:
                g4 = grp.tile([P, 2, NBLK, 4], BF16, tag="g4", name="g4_%d" % blk, align_bytes=64)
                grouped[blk] = g4
            tp = tpp.tile([P, 2, 2, P], F32, tag="tp", name="tp%d_%d" % (blk, r))
            tps[(blk, r)] = tp
            src = rows[blk][r].bitcast(F32)
            for g in range(2):
                for u in range(2):
                    nc.tensor.transpose(tp[:, g, u, :], src[:, 256 * g + u : 256 * (g + 1) : 2], ident[:])

        def E_(eng, blk, r):
            copy_on(
                eng,
                grouped[blk][:].bitcast(F32)[:, :, r * P : (r + 1) * P, :],
                tps[(blk, r)][:].rearrange("p g u r -> p g r u"),
            )

        def Q(blk, g):
            if g == 0:
                cd = keep.tile([P, 2, NBLK], U32, name="cd%d" % blk, align_bytes=64)
                pl = keep.tile([P, 2, NBLK], U8, name="pl%d" % blk, align_bytes=64)
                codes[blk], planes[blk] = cd, pl
            nc.vector.quantize_mx(
                out=codes[blk][:, g, :].bitcast(FP8X4),
                scales=planes[blk][:, g, :],
                in_=grouped[blk][:, g, :, :].rearrange("p f t -> p (f t)"),
            )

        def M(blk, tt):
            acc = accp.tile([P, NBLK], F32, tag="acc", name="acc%d_%d" % (blk, tt))
            accs[(blk, tt)] = acc
            for g in range(2):
                nc.tensor.matmul_mx(
                    out=acc[:],
                    lhsT=codes[0][:, g, tt * P : (tt + 1) * P].bitcast(FP8X4),
                    lhsT_scale=planes[0][:, g, tt * P : (tt + 1) * P],
                    rhs=codes[blk][:, g, :].bitcast(FP8X4),
                    rhs_scale=planes[blk][:, g, :],
                    start=(g == 0),
                    stop=(g == 1),
                )

        def A(blk, tt, h0=0, h1=4):
            w, c = divmod(blk - 1, 2)
            nc.vector.tensor_tensor(
                out=y[(w, tt // 2)][:, 4 * c + h0 : 4 * c + h1, tt % 2, :].rearrange("p h (e r) -> p h e r", r=4),
                in0=accs[(blk, tt)][:].rearrange("p (r h e) -> p h e r", r=4, h=4)[:, h0:h1, :, :],
                in1=bias[w][:, c * NBLK : (c + 1) * NBLK].rearrange("p (h e r) -> p h e r", h=4, r=4)[:, h0:h1, :, :],
                op=ALU.add,
            )

        def Sq(w, tt):
            junk = scr.tile([P, 8, P], F32, tag="junk", name="junk%d_%d" % (w, tt))
            nc.scalar.activation(
                out=junk[:], in_=y[(w, tt // 2)][:, :, tt % 2, :], func=ACT.Square, accum_out=ss[w][:, tt : tt + 1]
            )

        def N1(w, b):
            m = small.tile([P, 2], F32, name="n2_%d%d" % (w, b))
            nc.vector.tensor_scalar(
                out=m[:], in0=ss[w][:, 2 * b : 2 * b + 2], scalar1=1e-24, scalar2=None, op0=ALU.max
            )
            n2[(w, b)] = m

        def N2(w, b):
            n = small.tile([P, 2], F32, name="n3_%d%d" % (w, b))
            nc.scalar.activation(out=n[:], in_=n2[(w, b)][:], func=ACT.Sqrt)
            n2[(w, b)] = n

        def N3(w, b):
            n = small.tile([P, 2], F32, name="n4_%d%d" % (w, b))
            nc.vector.reciprocal(out=n[:], in_=n2[(w, b)][:])
            rn[(w, b)] = n

        def R(eng, w, tt):
            v = y[(w, tt // 2)][:, :, tt % 2, :]
            f = rn[(w, tt // 2)][:, tt % 2 : tt % 2 + 1]
            if eng == "V":
                nc.vector.tensor_scalar(out=v, in0=v, scalar1=f, scalar2=None, op0=ALU.mult)
            else:
                nc.scalar.activation(out=v, in_=v, func=ACT.Copy, scale=f)

        def St(w, b, h0, h1):
            h = slice(h0, h1)
            nc.sync.dma_start(
                out=outs[w][b, h].rearrange("h (p j) d -> p h (j d)", j=2),
                in_=y[(w, b)][:, h, :, :].rearrange("p h j d -> p h (j d)"),
            )


        units = [(2 * w + 1 + c, 2 * b + j) for w in range(2) for b in range(2) for c in range(2) for j in range(2)]
        units += [(5 + c, 2 * b + j) for c in range(2) for b in range(2) for j in range(2)]
        pe = [("warm",)]
        for blk in range(7):
            pe.extend([("T", blk, r) for r in range(4)])
            if blk < 3:
                pe.append(("bias", blk))
            else:
                pe.extend([("M",) + u for u in units[4 * (blk - 3) : 4 * (blk - 3) + 4]])
        pe.extend([("M",) + u for u in units[16:]])
        place = {op: i for i, op in enumerate(pe)}

        ops = {}
        queues = {"PE": [], "V": [], "S": [], "SP": []}

        def add(eng, key, name, deps, emit, takes=(), frees=()):
            ops[name] = (deps, emit, takes, frees, key)
            queues[eng].append((key, len(ops), name))

        VE = ((0, 1), (0, 3))
        BC = "VVV"
        RE = "VVVVVSVS"
        for op in pe:
            k = float(place[op])
            if op[0] == "warm":
                add("PE", k, op, (), lambda: warm(4), takes=("acc",), frees=("acc",))
            elif op[0] == "bias":
                w, eng = op[1], BC[op[1]]
                add("PE", k, op, (), lambda w=w: bmm(w), takes=("acc",))
                add(eng, k + 3.0, ("bc", w), (op,), lambda eng=eng, w=w: bc(eng, w), frees=("acc",))
            elif op[0] == "T":
                blk, r = op[1:]
                eng = "V" if (blk, r) in VE else "S"
                add("PE", k, op, (), lambda blk=blk, r=r: T(blk, r), takes=("tp", "grp") if r == 0 else ("tp",))
                add(eng, k + 3.0, ("E", blk, r), (op,), lambda eng=eng, blk=blk, r=r: E_(eng, blk, r), frees=("tp",))
            else:
                blk, tt = op[1:]
                w = (blk - 1) // 2
                add("PE", k, op, (("Q", 0, 1), ("Q", blk, 1)), lambda blk=blk, tt=tt: M(blk, tt), takes=("acc",))
                if (blk, tt) in units[-2:]:
                    for q in range(2):
                        add(
                            "V", place[("M",) + units[-1]] + 0.5 + 0.2 * q, ("A", blk, tt, q), (op, ("bc", w)),
                            lambda blk=blk, tt=tt, q=q: A(blk, tt, 2 * q, 2 * q + 2), frees=("acc",) if q else (),
                        )
                else:
                    add("V", k + 0.5, ("A", blk, tt), (op, ("bc", w)), lambda blk=blk, tt=tt: A(blk, tt), frees=("acc",))
        for blk in range(7):
            for g in range(2):
                add(
                    "V", max(place[("T", blk, r)] for r in range(4)) + 3.0 + 1.5 + 0.01 * g, ("Q", blk, g),
                    tuple(("E", blk, r) for r in range(4)), lambda blk=blk, g=g: Q(blk, g), frees=("grp",) if g else (),
                )
        for w in range(2):
            for b in range(2):
                for tt in (2 * b, 2 * b + 1):
                    srcs = (("A", 2 * w + 1, tt), ("A", 2 * w + 2, tt))
                    add("S", max(ops[s][4] for s in srcs) + 2.0, ("Sq", w, tt), srcs, lambda w=w, tt=tt: Sq(w, tt))
                k = ops[("Sq", w, 2 * b + 1)][4]
                add("V", k + 3.0, ("N1", w, b), (("Sq", w, 2 * b), ("Sq", w, 2 * b + 1)), lambda w=w, b=b: N1(w, b))
                add("S", k + 3.0, ("N2", w, b), (("N1", w, b),), lambda w=w, b=b: N2(w, b))
                add("V", k + 5.0, ("N3", w, b), (("N2", w, b),), lambda w=w, b=b: N3(w, b))
                for j in range(2):
                    tt = 2 * b + j
                    eng = RE[4 * w + tt]
                    add(eng, k + 5.0 + 0.1 + 1.0 * j, ("R", w, tt), (("N3", w, b),), lambda eng=eng, w=w, tt=tt: R(eng, w, tt))
                for c in range(2):
                    add("SP", k + 5.0 + 3.0 + 0.1 * c, ("St", w, b, c), (("R", w, 2 * b), ("R", w, 2 * b + 1)), lambda w=w, b=b, c=c: St(w, b, 4 * c, 4 * c + 4))
        for c in range(2):
            for b in range(2):
                if (5 + c, 2 * b + 1) == units[-1]:
                    for q in range(2):
                        srcs = (("A", 5 + c, 2 * b, q), ("A", 5 + c, 2 * b + 1, q))
                        add("SP", ops[srcs[1]][4] + 1.0, ("St", 2, b, c, q), srcs, lambda b=b, c=c, q=q: St(2, b, 4 * c + 2 * q, 4 * c + 2 * q + 2))
                else:
                    srcs = (("A", 5 + c, 2 * b), ("A", 5 + c, 2 * b + 1))
                    add("SP", ops[srcs[1]][4] + 1.0, ("St", 2, b, c), srcs, lambda b=b, c=c: St(2, b, 4 * c, 4 * c + 4))

        order = {e: [n for (k, i, n) in sorted(q)] for e, q in queues.items()}
        head = {e: 0 for e in order}
        done = set()
        bufs = {"tp": 4, "acc": 4, "grp": 3}
        held = {"tp": 0, "acc": 0, "grp": 0}
        left = len(ops)
        while left:
            moved = False
            for e in ("PE", "S", "V", "SP"):
                while head[e] < len(order[e]):
                    name = order[e][head[e]]
                    deps, emit, takes, frees, key = ops[name]
                    if not all(d in done for d in deps):
                        break
                    if not all(held[p] < bufs[p] for p in takes):
                        break
                    emit()
                    for p in takes:
                        held[p] += 1
                    for p in frees:
                        held[p] -= 1
                    done.add(name)
                    head[e] += 1
                    left -= 1
                    moved = True
            assert moved, "the orders of the engines block each other"
